import numpy as np
import ml_dtypes


def mxq(x, axis, fmt="e4m3"):
    dtype, down = {"e4m3": (ml_dtypes.float8_e4m3fn, 7), "e5m2": (ml_dtypes.float8_e5m2, 14)}[fmt]
    v = np.moveaxis(np.asarray(x, np.float32).astype(ml_dtypes.bfloat16).astype(np.float64), axis, -1)
    blocks = v.reshape(v.shape[:-1] + (-1, 32))
    amax = np.abs(blocks).max(-1, keepdims=True)
    byte = np.maximum(np.where(amax > 0, np.frexp(amax)[1] - 1 + 127, 0) - down, 1)
    scale = np.exp2(byte - 127.0)
    codes = (blocks / scale).astype(np.float32).astype(dtype).astype(np.float64)
    return np.moveaxis((codes * scale).reshape(v.shape), -1, axis)


WIDE = False


def mx_kscale(k):
    if not WIDE:
        return np.ones(k)
    levels = np.array([10, -10, 5, -5, 0])
    if k % 512:
        return np.exp2(np.random.permutation(np.resize(levels, k // 32))).repeat(32)
    a = np.empty((k // 512, 16))
    for p in range(k // 512):
        a[p, :8] = np.random.permutation(np.resize(levels, 8))
        for g in range(8):
            far = levels[np.abs(levels - a[p, g]) >= 10]
            a[p, g + 8] = far[np.random.randint(len(far))]
    return np.exp2(a.ravel()).repeat(32)


BF16 = ml_dtypes.bfloat16


def bf(x):
    return np.asarray(x, np.float32).astype(BF16)


def f64(x):
    return np.asarray(x).astype(np.float64)


N_V, N_E, N_F, D_IN, D_OUT = 1536, 3072, 2048, 128, 128
LIM = np.sqrt(6.0 / (D_IN + D_OUT))


def glorot():
    return np.random.uniform(-LIM, LIM, (D_IN, D_OUT))


def setup_inputs():
    se, sf = mx_kscale(N_E), mx_kscale(N_F)
    return {"xe": bf(np.random.standard_normal((N_E, D_IN)) / se[:, None]),
            "xf": bf(np.random.standard_normal((N_F, D_IN)) / sf[:, None]),
            "Ge2f": bf(np.random.standard_normal((N_F, N_E)) / np.sqrt(N_E) * se),
            "Gf2f": bf(np.random.standard_normal((N_F, N_F)) / np.sqrt(N_F) * sf),
            "We2f": bf(glorot()), "Wf2f": bf(glorot())}


def reference(xe, xf, Ge2f, Gf2f, We2f, Wf2f):
    he2f = f64(xe) @ f64(We2f)
    hf2f = f64(xf) @ f64(Wf2f)
    return (mxq(f64(Ge2f), 1, "e4m3") @ mxq(he2f, 0, "e4m3")) + (mxq(f64(Gf2f), 1, "e4m3") @ mxq(hf2f, 0, "e4m3"))

@@ -1,0 +1,185 @@
+from contextlib import ExitStack
+
+import concourse.mybir as mybir
+from concourse.masks import make_identity
+
+BF16 = mybir.dt.bfloat16
+F32 = mybir.dt.float32
+U32 = mybir.dt.uint32
+U8 = mybir.dt.uint8
+FP8X4 = mybir.dt.float8_e4m3fn_x4
+
+P = 128
+PACK = 4
+K_PASS = P * PACK
+N_E, N_F, D = 3072, 2048, 128
+E_PASSES = N_E // K_PASS
+F_PASSES = N_F // K_PASS
+PASSES = E_PASSES + F_PASSES
+WORDS_PASS = K_PASS // 2
+ROUNDS = N_F // P
+
+STEP_PASSES = 2
+STEPS = PASSES // STEP_PASSES
+STEP_COLS = STEP_PASSES * K_PASS
+STEP_WORDS = STEP_COLS // PACK
+
+X_AHEAD = 2
+G_BUFS = 14
+WORK_BANKS = 6
+
+FLOPS = 2 * N_F * (N_E + N_F) * D + 2 * (N_E + N_F) * D * D
+
+
+def tile_two_d_cxn_cmps_pb_kernel(tc, xe, xf, Ge2f, Gf2f, We2f, Wf2f, out):
+    nc = tc.nc
+    with ExitStack() as stack:
+        keep = stack.enter_context(tc.tile_pool(name="keep", bufs=1))
+        g_pool = stack.enter_context(tc.tile_pool(name="g", bufs=G_BUFS))
+        grouped_pool = stack.enter_context(tc.tile_pool(name="grouped", bufs=6))
+        quantised_pool = stack.enter_context(tc.tile_pool(name="quantised", bufs=4))
+        z_pool = stack.enter_context(tc.tile_pool(name="z", bufs=ROUNDS))
+        work = stack.enter_context(tc.psum_pool(name="work", bufs=WORK_BANKS))
+        sums = stack.enter_context(tc.psum_pool(name="sums", bufs=2))
+        stack.enter_context(tc.manual_schedule())
+
+        we_sb = keep.tile([P, D], BF16)
+        nc.sync.dma_start(out=we_sb[:], in_=We2f)
+        wf_sb = keep.tile([P, D], BF16)
+        nc.sync.dma_start(out=wf_sb[:], in_=Wf2f)
+        x_sb = keep.tile([P, PASSES * PACK, D], BF16)
+        x_passes = x_sb[:].rearrange("p (g t) d -> p g t d", t=PACK)
+        for x_dram, first_pass, passes in ((xe, 0, E_PASSES), (xf, E_PASSES, F_PASSES)):
+            passes_dram = x_dram.rearrange("(g p t) d -> p g t d", p=P, t=PACK)
+            for g in range(0, passes, STEP_PASSES):
+                nc.sync.dma_start(
+                    out=x_passes[:, first_pass + g : first_pass + g + STEP_PASSES],
+                    in_=passes_dram[:, g : g + STEP_PASSES],
+                )
+
+        def load_round(r):
+            rows = slice(r * P, (r + 1) * P)
+            ge = g_pool.tile([P, N_E], BF16)
+            nc.sync.dma_start(out=ge[:], in_=Ge2f[rows, :])
+            gf = g_pool.tile([P, N_F], BF16)
+            nc.sync.dma_start(out=gf[:], in_=Gf2f[rows, :])
+            return ge[:].bitcast(F32), gf[:].bitcast(F32)
+
+        g_words = {}
+        for r in range(G_BUFS):
+            g_words[r] = load_round(r)
+
+        ident_bf16 = keep.tile([P, P], BF16)
+        make_identity(nc, ident_bf16[:])
+        ident_f32 = keep.tile([P, P], F32)
+        make_identity(nc, ident_f32[:])
+
+        xT_sb = keep.tile([P, PASSES, PACK, P], BF16)
+        h_grouped = keep.tile([P, PASSES, D, PACK], BF16, align_bytes=64)
+        h_codes = keep.tile([P, PASSES * D], U32, align_bytes=64)
+        h_scales = keep.tile([P, PASSES * D], U8, align_bytes=64)
+
+        def copy_out(on_scalar, dst, src):
+            if on_scalar:
+                nc.scalar.copy(out=dst, in_=src)
+            else:
+                nc.vector.tensor_copy(out=dst, in_=src)
+
+        def transpose_x(g):
+            xT_bank = work.tile([P, PACK, P], BF16, tag="bank")
+            for t in range(PACK):
+                nc.tensor.transpose(xT_bank[:, t, :], x_sb[:, PACK * g + t, :], ident_bf16[:])
+            copy_out(g % 2 == 0, xT_sb[:, g], xT_bank[:])
+
+        def multiply_x(g):
+            w_sb = we_sb if g < E_PASSES else wf_sb
+            h_bank = work.tile([P, PACK, D], F32, tag="bank")
+            for t in range(PACK):
+                nc.tensor.matmul(
+                    h_bank[:, t, :], lhsT=xT_sb[:, g, t, :], rhs=w_sb[:], start=True, stop=True
+                )
+            copy_out(g % 2 == 1, h_grouped[:, g], h_bank[:].rearrange("p t d -> p d t"))
+
+        def quantise_h(c):
+            cols = slice(c * STEP_WORDS, (c + 1) * STEP_WORDS)
+            nc.vector.quantize_mx(
+                out=h_codes[:, cols].bitcast(FP8X4),
+                scales=h_scales[:, cols],
+                in_=h_grouped[:, c * STEP_PASSES : (c + 1) * STEP_PASSES].rearrange(
+                    "p g d t -> p (g d t)"
+                ),
+            )
+
+        for g in range(X_AHEAD):
+            transpose_x(g)
+        for g in range(PASSES):
+            if g + X_AHEAD < PASSES:
+                transpose_x(g + X_AHEAD)
+            multiply_x(g)
+            if g % STEP_PASSES == STEP_PASSES - 1 and g // STEP_PASSES >= 1:
+                quantise_h(g // STEP_PASSES - 1)
+        quantise_h(STEPS - 1)
+
+        quantised = {}
+        grouped_of = {}
+
+        def transpose_step(r, c):
+            ge_words, gf_words = g_words[r]
+            bank = work.tile([P, STEP_PASSES, 2, P], F32, tag="bank")
+            for i in range(STEP_PASSES):
+                g = c * STEP_PASSES + i
+                words, g_local = (ge_words, g) if g < E_PASSES else (gf_words, g - E_PASSES)
+                for u in range(2):
+                    first = g_local * WORDS_PASS
+                    nc.tensor.transpose(
+                        bank[:, i, u, :], words[:, first + u : first + WORDS_PASS : 2], ident_f32[:]
+                    )
+            grouped = grouped_pool.tile([P, STEP_COLS], BF16, align_bytes=64)
+            grouped_of[(r, c)] = grouped
+            dst = grouped[:].bitcast(F32).rearrange("p (i r u) -> p i r u", i=STEP_PASSES, u=2)
+            copy_out(c != 0, dst, bank[:].rearrange("p i u r -> p i r u"))
+
+        def quantise_step(r, c):
+            codes, scales = quantised[r]
+            cols = slice(c * STEP_WORDS, (c + 1) * STEP_WORDS)
+            nc.vector.quantize_mx(
+                out=codes[:, cols].bitcast(FP8X4), scales=scales[:, cols], in_=grouped_of[(r, c)][:]
+            )
+
+        def transpose_round(r):
+            codes = quantised_pool.tile([P, PASSES * P], U32, align_bytes=64)
+            scales = quantised_pool.tile([P, PASSES * P], U8, align_bytes=64)
+            quantised[r] = (codes, scales)
+            for c in range(STEPS):
+                transpose_step(r, c)
+                if c >= 1:
+                    quantise_step(r, c - 1)
+                elif r >= 1:
+                    quantise_step(r - 1, STEPS - 1)
+            if r + G_BUFS < ROUNDS:
+                g_words[r + G_BUFS] = load_round(r + G_BUFS)
+
+        def multiply_round(r):
+            codes, scales = quantised[r]
+            acc = sums.tile([P, D], F32)
+            for g in range(PASSES):
+                cols = slice(g * P, (g + 1) * P)
+                nc.tensor.matmul_mx(
+                    out=acc[:],
+                    lhsT=codes[:, cols].bitcast(FP8X4),
+                    lhsT_scale=scales[:, cols],
+                    rhs=h_codes[:, cols].bitcast(FP8X4),
+                    rhs_scale=h_scales[:, cols],
+                    start=(g == 0),
+                    stop=(g == PASSES - 1),
+                )
+            z = z_pool.tile([P, D], F32)
+            copy_out(r % 2 == 1, z[:], acc[:])
+            nc.sync.dma_start(out=out[r * P : (r + 1) * P, :], in_=z[:])
+
+        for r in range(ROUNDS):
+            transpose_round(r)
+            if r >= 1:
+                multiply_round(r - 1)
+        quantise_step(ROUNDS - 1, STEPS - 1)
+        multiply_round(ROUNDS - 1)

@@ -25,7 +25,10 @@ STEP_COLS = STEP_PASSES * K_PASS
 STEP_WORDS = STEP_COLS // PACK
 
 X_AHEAD = 2
-G_BUFS = 14
+SORTED_STEPS = 3
+SORT_AHEAD = 3
+G_START = 6
+G_BUFS = 12
 WORK_BANKS = 6
 
 FLOPS = 2 * N_F * (N_E + N_F) * D + 2 * (N_E + N_F) * D * D
@@ -36,6 +39,7 @@ def tile_two_d_cxn_cmps_pb_kernel(tc, xe, xf, Ge2f, Gf2f, We2f, Wf2f, out):
     with ExitStack() as stack:
         keep = stack.enter_context(tc.tile_pool(name="keep", bufs=1))
         g_pool = stack.enter_context(tc.tile_pool(name="g", bufs=G_BUFS))
+        sorted_pool = stack.enter_context(tc.tile_pool(name="sorted", bufs=6))
         grouped_pool = stack.enter_context(tc.tile_pool(name="grouped", bufs=6))
         quantised_pool = stack.enter_context(tc.tile_pool(name="quantised", bufs=4))
         z_pool = stack.enter_context(tc.tile_pool(name="z", bufs=ROUNDS))
@@ -110,54 +114,55 @@ def tile_two_d_cxn_cmps_pb_kernel(tc, xe, xf, Ge2f, Gf2f, We2f, Wf2f, out):
                 ),
             )
 
-        for g in range(X_AHEAD):
-            transpose_x(g)
-        for g in range(PASSES):
-            if g + X_AHEAD < PASSES:
-                transpose_x(g + X_AHEAD)
-            multiply_x(g)
-            if g % STEP_PASSES == STEP_PASSES - 1 and g // STEP_PASSES >= 1:
-                quantise_h(g // STEP_PASSES - 1)
-        quantise_h(STEPS - 1)
-
         quantised = {}
+        sorted_words = {}
         grouped_of = {}
 
-        def transpose_step(r, c):
+        def words_of(s):
+            r, c = divmod(s, STEPS)
             ge_words, gf_words = g_words[r]
+            first = c * STEP_PASSES
+            words = ge_words if first < E_PASSES else gf_words
+            local = first if first < E_PASSES else first - E_PASSES
+            return words[:, local * WORDS_PASS : (local + STEP_PASSES) * WORDS_PASS]
+
+        def is_sorted(s):
+            return s % STEPS < SORTED_STEPS
+
+        def sort_words(s):
+            tile = sorted_pool.tile([P, STEP_PASSES * WORDS_PASS], F32)
+            sorted_words[s] = tile
+            nc.vector.tensor_copy(
+                out=tile[:].rearrange("p (g u w) -> p g u w", g=STEP_PASSES, u=2),
+                in_=words_of(s).rearrange("p (g w u) -> p g u w", g=STEP_PASSES, u=2),
+            )
+
+        def transpose_step(s):
             bank = work.tile([P, STEP_PASSES, 2, P], F32, tag="bank")
             for i in range(STEP_PASSES):
-                g = c * STEP_PASSES + i
-                words, g_local = (ge_words, g) if g < E_PASSES else (gf_words, g - E_PASSES)
                 for u in range(2):
-                    first = g_local * WORDS_PASS
-                    nc.tensor.transpose(
-                        bank[:, i, u, :], words[:, first + u : first + WORDS_PASS : 2], ident_f32[:]
-                    )
+                    first = i * WORDS_PASS
+                    if is_sorted(s):
+                        src = sorted_words[s][:, first + u * P : first + (u + 1) * P]
+                    else:
+                        src = words_of(s)[:, first + u : first + WORDS_PASS : 2]
+                    nc.tensor.transpose(bank[:, i, u, :], src, ident_f32[:])
             grouped = grouped_pool.tile([P, STEP_COLS], BF16, align_bytes=64)
-            grouped_of[(r, c)] = grouped
+            grouped_of[s] = grouped
             dst = grouped[:].bitcast(F32).rearrange("p (i r u) -> p i r u", i=STEP_PASSES, u=2)
-            copy_out(c != 0, dst, bank[:].rearrange("p i u r -> p i r u"))
+            copy_out(True, dst, bank[:].rearrange("p i u r -> p i r u"))
 
-        def quantise_step(r, c):
+        def quantise_step(s):
+            r, c = divmod(s, STEPS)
+            if c == 0:
+                codes = quantised_pool.tile([P, PASSES * P], U32, align_bytes=64)
+                scales = quantised_pool.tile([P, PASSES * P], U8, align_bytes=64)
+                quantised[r] = (codes, scales)
             codes, scales = quantised[r]
             cols = slice(c * STEP_WORDS, (c + 1) * STEP_WORDS)
             nc.vector.quantize_mx(
-                out=codes[:, cols].bitcast(FP8X4), scales=scales[:, cols], in_=grouped_of[(r, c)][:]
+                out=codes[:, cols].bitcast(FP8X4), scales=scales[:, cols], in_=grouped_of[s][:]
             )
-
-        def transpose_round(r):
-            codes = quantised_pool.tile([P, PASSES * P], U32, align_bytes=64)
-            scales = quantised_pool.tile([P, PASSES * P], U8, align_bytes=64)
-            quantised[r] = (codes, scales)
-            for c in range(STEPS):
-                transpose_step(r, c)
-                if c >= 1:
-                    quantise_step(r, c - 1)
-                elif r >= 1:
-                    quantise_step(r - 1, STEPS - 1)
-            if r + G_BUFS < ROUNDS:
-                g_words[r + G_BUFS] = load_round(r + G_BUFS)
 
         def multiply_round(r):
             codes, scales = quantised[r]
@@ -174,12 +179,35 @@ def tile_two_d_cxn_cmps_pb_kernel(tc, xe, xf, Ge2f, Gf2f, We2f, Wf2f, out):
                     stop=(g == PASSES - 1),
                 )
             z = z_pool.tile([P, D], F32)
-            copy_out(r % 2 == 1, z[:], acc[:])
+            copy_out(False, z[:], acc[:])
             nc.sync.dma_start(out=out[r * P : (r + 1) * P, :], in_=z[:])
 
-        for r in range(ROUNDS):
-            transpose_round(r)
-            if r >= 1:
-                multiply_round(r - 1)
-        quantise_step(ROUNDS - 1, STEPS - 1)
+        def advance(s):
+            if s + SORT_AHEAD < ROUNDS * STEPS and is_sorted(s + SORT_AHEAD):
+                sort_words(s + SORT_AHEAD)
+            if s >= 0:
+                transpose_step(s)
+            if s >= 1:
+                quantise_step(s - 1)
+            r, c = divmod(s, STEPS)
+            if r >= 0 and c == STEPS - 1:
+                if r + G_BUFS < ROUNDS:
+                    g_words[r + G_BUFS] = load_round(r + G_BUFS)
+                if r >= 1:
+                    multiply_round(r - 1)
+
+        for g in range(X_AHEAD):
+            transpose_x(g)
+        for g in range(PASSES):
+            if g + X_AHEAD < PASSES:
+                transpose_x(g + X_AHEAD)
+            multiply_x(g)
+            if g % STEP_PASSES == STEP_PASSES - 1 and g // STEP_PASSES >= 1:
+                quantise_h(g // STEP_PASSES - 1)
+            if g >= G_START - SORT_AHEAD:
+                advance(g - G_START)
+        quantise_h(STEPS - 1)
+        for s in range(PASSES - G_START, ROUNDS * STEPS):
+            advance(s)
+        quantise_step(ROUNDS * STEPS - 1)
         multiply_round(ROUNDS - 1)

@@ -25,8 +25,7 @@ STEP_COLS = STEP_PASSES * K_PASS
 STEP_WORDS = STEP_COLS // PACK
 
 X_AHEAD = 2
-SORTED_STEPS = 3
-SORT_AHEAD = 3
+SORT_AHEAD = 4
 G_START = 6
 G_BUFS = 12
 WORK_BANKS = 6
@@ -39,7 +38,7 @@ def tile_two_d_cxn_cmps_pb_kernel(tc, xe, xf, Ge2f, Gf2f, We2f, Wf2f, out):
     with ExitStack() as stack:
         keep = stack.enter_context(tc.tile_pool(name="keep", bufs=1))
         g_pool = stack.enter_context(tc.tile_pool(name="g", bufs=G_BUFS))
-        sorted_pool = stack.enter_context(tc.tile_pool(name="sorted", bufs=6))
+        sorted_pool = stack.enter_context(tc.tile_pool(name="sorted", bufs=3))
         grouped_pool = stack.enter_context(tc.tile_pool(name="grouped", bufs=6))
         quantised_pool = stack.enter_context(tc.tile_pool(name="quantised", bufs=4))
         z_pool = stack.enter_context(tc.tile_pool(name="z", bufs=ROUNDS))
@@ -118,35 +117,29 @@ def tile_two_d_cxn_cmps_pb_kernel(tc, xe, xf, Ge2f, Gf2f, We2f, Wf2f, out):
         sorted_words = {}
         grouped_of = {}
 
-        def words_of(s):
-            r, c = divmod(s, STEPS)
-            ge_words, gf_words = g_words[r]
-            first = c * STEP_PASSES
-            words = ge_words if first < E_PASSES else gf_words
-            local = first if first < E_PASSES else first - E_PASSES
-            return words[:, local * WORDS_PASS : (local + STEP_PASSES) * WORDS_PASS]
-
-        def is_sorted(s):
-            return s % STEPS < SORTED_STEPS
-
-        def sort_words(s):
-            tile = sorted_pool.tile([P, STEP_PASSES * WORDS_PASS], F32)
-            sorted_words[s] = tile
+        def sort_words(r):
+            tile = sorted_pool.tile([P, E_PASSES * WORDS_PASS], F32)
+            sorted_words[r] = tile
             nc.vector.tensor_copy(
-                out=tile[:].rearrange("p (g u w) -> p g u w", g=STEP_PASSES, u=2),
-                in_=words_of(s).rearrange("p (g w u) -> p g u w", g=STEP_PASSES, u=2),
+                out=tile[:].rearrange("p (g u w) -> p g u w", g=E_PASSES, u=2),
+                in_=g_words[r][0].rearrange("p (g w u) -> p g u w", g=E_PASSES, u=2),
             )
 
+        def words_of(r, g, u):
+            if g < E_PASSES:
+                first = (2 * g + u) * P
+                return sorted_words[r][:, first : first + P]
+            first = (g - E_PASSES) * WORDS_PASS
+            return g_words[r][1][:, first + u : first + WORDS_PASS : 2]
+
         def transpose_step(s):
+            r, c = divmod(s, STEPS)
             bank = work.tile([P, STEP_PASSES, 2, P], F32, tag="bank")
             for i in range(STEP_PASSES):
                 for u in range(2):
-                    first = i * WORDS_PASS
-                    if is_sorted(s):
-                        src = sorted_words[s][:, first + u * P : first + (u + 1) * P]
-                    else:
-                        src = words_of(s)[:, first + u : first + WORDS_PASS : 2]
-                    nc.tensor.transpose(bank[:, i, u, :], src, ident_f32[:])
+                    nc.tensor.transpose(
+                        bank[:, i, u, :], words_of(r, c * STEP_PASSES + i, u), ident_f32[:]
+                    )
             grouped = grouped_pool.tile([P, STEP_COLS], BF16, align_bytes=64)
             grouped_of[s] = grouped
             dst = grouped[:].bitcast(F32).rearrange("p (i r u) -> p i r u", i=STEP_PASSES, u=2)
@@ -183,8 +176,8 @@ def tile_two_d_cxn_cmps_pb_kernel(tc, xe, xf, Ge2f, Gf2f, We2f, Wf2f, out):
             nc.sync.dma_start(out=out[r * P : (r + 1) * P, :], in_=z[:])
 
         def advance(s):
-            if s + SORT_AHEAD < ROUNDS * STEPS and is_sorted(s + SORT_AHEAD):
-                sort_words(s + SORT_AHEAD)
+            if s + SORT_AHEAD < ROUNDS * STEPS and (s + SORT_AHEAD) % STEPS == 0:
+                sort_words((s + SORT_AHEAD) // STEPS)
             if s >= 0:
                 transpose_step(s)
             if s >= 1:

@@ -20,13 +20,18 @@ WORDS_PASS = K_PASS // 2
 ROUNDS = N_F // P
 
 STEP_PASSES = 2
-STEPS = PASSES // STEP_PASSES
+ROUND_STEPS = PASSES // STEP_PASSES
+STEPS = ROUNDS * ROUND_STEPS
 STEP_COLS = STEP_PASSES * K_PASS
 STEP_WORDS = STEP_COLS // PACK
+UNIT_STEPS = 2
+ALONE_STEPS = 4
 
 X_AHEAD = 2
-SORT_AHEAD = 4
 G_START = 6
+SORT_AHEAD = 4
+MX_ROUNDS = 2
+MX_LAG = 5
 G_BUFS = 12
 WORK_BANKS = 6
 
@@ -38,35 +43,40 @@ def tile_two_d_cxn_cmps_pb_kernel(tc, xe, xf, Ge2f, Gf2f, We2f, Wf2f, out):
     with ExitStack() as stack:
         keep = stack.enter_context(tc.tile_pool(name="keep", bufs=1))
         g_pool = stack.enter_context(tc.tile_pool(name="g", bufs=G_BUFS))
-        sorted_pool = stack.enter_context(tc.tile_pool(name="sorted", bufs=3))
-        grouped_pool = stack.enter_context(tc.tile_pool(name="grouped", bufs=6))
-        quantised_pool = stack.enter_context(tc.tile_pool(name="quantised", bufs=4))
+        sorted_pool = stack.enter_context(tc.tile_pool(name="sorted", bufs=2))
+        grouped_pool = stack.enter_context(tc.tile_pool(name="grouped", bufs=4))
+        quantised_pool = stack.enter_context(tc.tile_pool(name="quantised", bufs=12))
         z_pool = stack.enter_context(tc.tile_pool(name="z", bufs=ROUNDS))
         work = stack.enter_context(tc.psum_pool(name="work", bufs=WORK_BANKS))
         sums = stack.enter_context(tc.psum_pool(name="sums", bufs=2))
         stack.enter_context(tc.manual_schedule())
 
+        x_sb = keep.tile([P, PASSES * PACK, D], BF16)
+        x_passes = x_sb[:].rearrange("p (g t) d -> p g t d", t=PACK)
+        xe_passes = xe.rearrange("(g p t) d -> p g t d", p=P, t=PACK)
+        xf_passes = xf.rearrange("(g p t) d -> p g t d", p=P, t=PACK)
+
+        def load_x(g, passes):
+            src, first = (xe_passes, g) if g < E_PASSES else (xf_passes, g - E_PASSES)
+            nc.sync.dma_start(
+                out=x_passes[:, g : g + passes], in_=src[:, first : first + passes]
+            )
+
+        load_x(0, 1)
         we_sb = keep.tile([P, D], BF16)
         nc.sync.dma_start(out=we_sb[:], in_=We2f)
         wf_sb = keep.tile([P, D], BF16)
         nc.sync.dma_start(out=wf_sb[:], in_=Wf2f)
-        x_sb = keep.tile([P, PASSES * PACK, D], BF16)
-        x_passes = x_sb[:].rearrange("p (g t) d -> p g t d", t=PACK)
-        for x_dram, first_pass, passes in ((xe, 0, E_PASSES), (xf, E_PASSES, F_PASSES)):
-            passes_dram = x_dram.rearrange("(g p t) d -> p g t d", p=P, t=PACK)
-            for g in range(0, passes, STEP_PASSES):
-                nc.sync.dma_start(
-                    out=x_passes[:, first_pass + g : first_pass + g + STEP_PASSES],
-                    in_=passes_dram[:, g : g + STEP_PASSES],
-                )
+        load_x(1, 1)
+        for g in range(2, PASSES, 2):
+            load_x(g, 2)
 
         def load_round(r):
             rows = slice(r * P, (r + 1) * P)
-            ge = g_pool.tile([P, N_E], BF16)
-            nc.sync.dma_start(out=ge[:], in_=Ge2f[rows, :])
-            gf = g_pool.tile([P, N_F], BF16)
-            nc.sync.dma_start(out=gf[:], in_=Gf2f[rows, :])
-            return ge[:].bitcast(F32), gf[:].bitcast(F32)
+            g_tile = g_pool.tile([P, N_E + N_F], BF16)
+            nc.sync.dma_start(out=g_tile[:, :N_E], in_=Ge2f[rows, :])
+            nc.sync.dma_start(out=g_tile[:, N_E:], in_=Gf2f[rows, :])
+            return g_tile[:].bitcast(F32)
 
         g_words = {}
         for r in range(G_BUFS):
@@ -113,81 +123,99 @@ def tile_two_d_cxn_cmps_pb_kernel(tc, xe, xf, Ge2f, Gf2f, We2f, Wf2f, out):
                 ),
             )
 
-        quantised = {}
+        units = []
+        unit_of = {}
+        for s in range(STEPS):
+            first, steps = units[-1] if units else (0, UNIT_STEPS)
+            if not units or steps == UNIT_STEPS or s >= STEPS - ALONE_STEPS:
+                units.append((s, 1))
+            else:
+                units[-1] = (first, steps + 1)
+            unit_of[s] = (len(units) - 1, s - units[-1][0])
         sorted_words = {}
         grouped_of = {}
+        quantised = {}
 
         def sort_words(r):
             tile = sorted_pool.tile([P, E_PASSES * WORDS_PASS], F32)
             sorted_words[r] = tile
             nc.vector.tensor_copy(
                 out=tile[:].rearrange("p (g u w) -> p g u w", g=E_PASSES, u=2),
-                in_=g_words[r][0].rearrange("p (g w u) -> p g u w", g=E_PASSES, u=2),
+                in_=g_words[r][:, : E_PASSES * WORDS_PASS].rearrange(
+                    "p (g w u) -> p g u w", g=E_PASSES, u=2
+                ),
             )
 
         def words_of(r, g, u):
             if g < E_PASSES:
                 first = (2 * g + u) * P
                 return sorted_words[r][:, first : first + P]
-            first = (g - E_PASSES) * WORDS_PASS
-            return g_words[r][1][:, first + u : first + WORDS_PASS : 2]
+            return g_words[r][:, g * WORDS_PASS + u : (g + 1) * WORDS_PASS : 2]
 
         def transpose_step(s):
-            r, c = divmod(s, STEPS)
+            r, c = divmod(s, ROUND_STEPS)
             bank = work.tile([P, STEP_PASSES, 2, P], F32, tag="bank")
             for i in range(STEP_PASSES):
                 for u in range(2):
                     nc.tensor.transpose(
                         bank[:, i, u, :], words_of(r, c * STEP_PASSES + i, u), ident_f32[:]
                     )
-            grouped = grouped_pool.tile([P, STEP_COLS], BF16, align_bytes=64)
-            grouped_of[s] = grouped
-            dst = grouped[:].bitcast(F32).rearrange("p (i r u) -> p i r u", i=STEP_PASSES, u=2)
-            copy_out(True, dst, bank[:].rearrange("p i u r -> p i r u"))
+            j, place = unit_of[s]
+            if place == 0:
+                grouped = grouped_pool.tile([P, units[j][1] * STEP_COLS], BF16, align_bytes=64)
+                grouped_of[j] = grouped
+            cols = slice(place * STEP_COLS, (place + 1) * STEP_COLS)
+            dst = grouped_of[j][:, cols].bitcast(F32)
+            dst = dst.rearrange("p (i r u) -> p i r u", i=STEP_PASSES, u=2)
+            nc.scalar.copy(out=dst, in_=bank[:].rearrange("p i u r -> p i r u"))
 
-        def quantise_step(s):
-            r, c = divmod(s, STEPS)
-            if c == 0:
-                codes = quantised_pool.tile([P, PASSES * P], U32, align_bytes=64)
-                scales = quantised_pool.tile([P, PASSES * P], U8, align_bytes=64)
-                quantised[r] = (codes, scales)
-            codes, scales = quantised[r]
-            cols = slice(c * STEP_WORDS, (c + 1) * STEP_WORDS)
+        def quantise_unit(j):
+            words = units[j][1] * STEP_WORDS
+            codes = quantised_pool.tile([P, words], U32, align_bytes=64)
+            scales = quantised_pool.tile([P, words], U8, align_bytes=64)
+            quantised[j] = (codes, scales)
             nc.vector.quantize_mx(
-                out=codes[:, cols].bitcast(FP8X4), scales=scales[:, cols], in_=grouped_of[s][:]
+                out=codes[:].bitcast(FP8X4), scales=scales[:], in_=grouped_of[j][:]
             )
 
         def multiply_round(r):
-            codes, scales = quantised[r]
             acc = sums.tile([P, D], F32)
             for g in range(PASSES):
-                cols = slice(g * P, (g + 1) * P)
+                c, i = divmod(g, STEP_PASSES)
+                j, place = unit_of[r * ROUND_STEPS + c]
+                codes, scales = quantised[j]
+                first = (place * STEP_PASSES + i) * P
+                h_cols = slice(g * D, (g + 1) * D)
                 nc.tensor.matmul_mx(
                     out=acc[:],
-                    lhsT=codes[:, cols].bitcast(FP8X4),
-                    lhsT_scale=scales[:, cols],
-                    rhs=h_codes[:, cols].bitcast(FP8X4),
-                    rhs_scale=h_scales[:, cols],
+                    lhsT=codes[:, first : first + P].bitcast(FP8X4),
+                    lhsT_scale=scales[:, first : first + P],
+                    rhs=h_codes[:, h_cols].bitcast(FP8X4),
+                    rhs_scale=h_scales[:, h_cols],
                     start=(g == 0),
                     stop=(g == PASSES - 1),
                 )
             z = z_pool.tile([P, D], F32)
-            copy_out(False, z[:], acc[:])
+            nc.scalar.copy(out=z[:], in_=acc[:])
             nc.sync.dma_start(out=out[r * P : (r + 1) * P, :], in_=z[:])
 
         def advance(s):
-            if s + SORT_AHEAD < ROUNDS * STEPS and (s + SORT_AHEAD) % STEPS == 0:
-                sort_words((s + SORT_AHEAD) // STEPS)
+            r, c = divmod(s + SORT_AHEAD, ROUND_STEPS)
+            if r < ROUNDS and c == 0:
+                sort_words(r)
             if s >= 0:
                 transpose_step(s)
             if s >= 1:
-                quantise_step(s - 1)
-            r, c = divmod(s, STEPS)
-            if r >= 0 and c == STEPS - 1:
-                if r + G_BUFS < ROUNDS:
-                    g_words[r + G_BUFS] = load_round(r + G_BUFS)
-                if r >= 1:
-                    multiply_round(r - 1)
+                j, place = unit_of[s - 1]
+                if place == units[j][1] - 1:
+                    quantise_unit(j)
+            rounds, c = divmod(s - MX_LAG + 1, ROUND_STEPS)
+            if rounds > 0 and c == 0 and rounds % MX_ROUNDS == 0:
+                for r in range(rounds - MX_ROUNDS, rounds):
+                    multiply_round(r)
+            r, c = divmod(s, ROUND_STEPS)
+            if r >= 0 and c == ROUND_STEPS - 1 and r + G_BUFS < ROUNDS:
+                g_words[r + G_BUFS] = load_round(r + G_BUFS)
 
         for g in range(X_AHEAD):
             transpose_x(g)
@@ -199,8 +227,9 @@ def tile_two_d_cxn_cmps_pb_kernel(tc, xe, xf, Ge2f, Gf2f, We2f, Wf2f, out):
                 quantise_h(g // STEP_PASSES - 1)
             if g >= G_START - SORT_AHEAD:
                 advance(g - G_START)
-        quantise_h(STEPS - 1)
-        for s in range(PASSES - G_START, ROUNDS * STEPS):
+        quantise_h(PASSES // STEP_PASSES - 1)
+        for s in range(PASSES - G_START, STEPS):
             advance(s)
-        quantise_step(ROUNDS * STEPS - 1)
-        multiply_round(ROUNDS - 1)
+        quantise_unit(len(units) - 1)
+        for r in range((STEPS - MX_LAG) // (MX_ROUNDS * ROUND_STEPS) * MX_ROUNDS, ROUNDS):
+            multiply_round(r)

@@ -28,10 +28,9 @@ UNIT_STEPS = 2
 ALONE_STEPS = 4
 
 X_AHEAD = 2
-G_START = 6
-SORT_AHEAD = 4
-MX_ROUNDS = 2
-MX_LAG = 5
+G_START = 7
+SORT_AHEAD = 5
+MX_LAG = 8
 G_BUFS = 12
 WORK_BANKS = 6
 
@@ -45,7 +44,7 @@ def tile_two_d_cxn_cmps_pb_kernel(tc, xe, xf, Ge2f, Gf2f, We2f, Wf2f, out):
         g_pool = stack.enter_context(tc.tile_pool(name="g", bufs=G_BUFS))
         sorted_pool = stack.enter_context(tc.tile_pool(name="sorted", bufs=2))
         grouped_pool = stack.enter_context(tc.tile_pool(name="grouped", bufs=4))
-        quantised_pool = stack.enter_context(tc.tile_pool(name="quantised", bufs=12))
+        quantised_pool = stack.enter_context(tc.tile_pool(name="quantised", bufs=10))
         z_pool = stack.enter_context(tc.tile_pool(name="z", bufs=ROUNDS))
         work = stack.enter_context(tc.psum_pool(name="work", bufs=WORK_BANKS))
         sums = stack.enter_context(tc.psum_pool(name="sums", bufs=2))
@@ -102,7 +101,7 @@ def tile_two_d_cxn_cmps_pb_kernel(tc, xe, xf, Ge2f, Gf2f, We2f, Wf2f, out):
             xT_bank = work.tile([P, PACK, P], BF16, tag="bank")
             for t in range(PACK):
                 nc.tensor.transpose(xT_bank[:, t, :], x_sb[:, PACK * g + t, :], ident_bf16[:])
-            copy_out(g % 2 == 0, xT_sb[:, g], xT_bank[:])
+            nc.scalar.copy(out=xT_sb[:, g], in_=xT_bank[:])
 
         def multiply_x(g):
             w_sb = we_sb if g < E_PASSES else wf_sb
@@ -136,18 +135,22 @@ def tile_two_d_cxn_cmps_pb_kernel(tc, xe, xf, Ge2f, Gf2f, We2f, Wf2f, out):
         grouped_of = {}
         quantised = {}
 
+        def sorted_passes(r):
+            return 6 if r < 2 else 8
+
         def sort_words(r):
-            tile = sorted_pool.tile([P, E_PASSES * WORDS_PASS], F32)
+            passes = sorted_passes(r)
+            tile = sorted_pool.tile([P, passes * WORDS_PASS], F32)
             sorted_words[r] = tile
             nc.vector.tensor_copy(
-                out=tile[:].rearrange("p (g u w) -> p g u w", g=E_PASSES, u=2),
-                in_=g_words[r][:, : E_PASSES * WORDS_PASS].rearrange(
-                    "p (g w u) -> p g u w", g=E_PASSES, u=2
+                out=tile[:].rearrange("p (g u w) -> p g u w", g=passes, u=2),
+                in_=g_words[r][:, : passes * WORDS_PASS].rearrange(
+                    "p (g w u) -> p g u w", g=passes, u=2
                 ),
             )
 
         def words_of(r, g, u):
-            if g < E_PASSES:
+            if g < sorted_passes(r):
                 first = (2 * g + u) * P
                 return sorted_words[r][:, first : first + P]
             return g_words[r][:, g * WORDS_PASS + u : (g + 1) * WORDS_PASS : 2]
@@ -196,7 +199,7 @@ def tile_two_d_cxn_cmps_pb_kernel(tc, xe, xf, Ge2f, Gf2f, We2f, Wf2f, out):
                     stop=(g == PASSES - 1),
                 )
             z = z_pool.tile([P, D], F32)
-            nc.scalar.copy(out=z[:], in_=acc[:])
+            copy_out(r % 2 == 0, z[:], acc[:])
             nc.sync.dma_start(out=out[r * P : (r + 1) * P, :], in_=z[:])
 
         def advance(s):
@@ -209,10 +212,9 @@ def tile_two_d_cxn_cmps_pb_kernel(tc, xe, xf, Ge2f, Gf2f, We2f, Wf2f, out):
                 j, place = unit_of[s - 1]
                 if place == units[j][1] - 1:
                     quantise_unit(j)
-            rounds, c = divmod(s - MX_LAG + 1, ROUND_STEPS)
-            if rounds > 0 and c == 0 and rounds % MX_ROUNDS == 0:
-                for r in range(rounds - MX_ROUNDS, rounds):
-                    multiply_round(r)
+            r, c = divmod(s - MX_LAG, ROUND_STEPS)
+            if r >= 0 and c == ROUND_STEPS - 1:
+                multiply_round(r)
             r, c = divmod(s, ROUND_STEPS)
             if r >= 0 and c == ROUND_STEPS - 1 and r + G_BUFS < ROUNDS:
                 g_words[r + G_BUFS] = load_round(r + G_BUFS)
@@ -231,5 +233,5 @@ def tile_two_d_cxn_cmps_pb_kernel(tc, xe, xf, Ge2f, Gf2f, We2f, Wf2f, out):
         for s in range(PASSES - G_START, STEPS):
             advance(s)
         quantise_unit(len(units) - 1)
-        for r in range((STEPS - MX_LAG) // (MX_ROUNDS * ROUND_STEPS) * MX_ROUNDS, ROUNDS):
+        for r in range((STEPS - MX_LAG) // ROUND_STEPS, ROUNDS):
             multiply_round(r)

@@ -30,6 +30,7 @@ ALONE_STEPS = 4
 X_AHEAD = 2
 G_START = 7
 SORT_AHEAD = 5
+SORTS = {1: (2, E_PASSES), 3: (E_PASSES, PASSES)}
 MX_LAG = 8
 G_BUFS = 12
 WORK_BANKS = 6
@@ -42,7 +43,7 @@ def tile_two_d_cxn_cmps_pb_kernel(tc, xe, xf, Ge2f, Gf2f, We2f, Wf2f, out):
     with ExitStack() as stack:
         keep = stack.enter_context(tc.tile_pool(name="keep", bufs=1))
         g_pool = stack.enter_context(tc.tile_pool(name="g", bufs=G_BUFS))
-        sorted_pool = stack.enter_context(tc.tile_pool(name="sorted", bufs=2))
+        sorted_pool = stack.enter_context(tc.tile_pool(name="sorted", bufs=4))
         grouped_pool = stack.enter_context(tc.tile_pool(name="grouped", bufs=4))
         quantised_pool = stack.enter_context(tc.tile_pool(name="quantised", bufs=10))
         z_pool = stack.enter_context(tc.tile_pool(name="z", bufs=ROUNDS))
@@ -101,7 +102,7 @@ def tile_two_d_cxn_cmps_pb_kernel(tc, xe, xf, Ge2f, Gf2f, We2f, Wf2f, out):
             xT_bank = work.tile([P, PACK, P], BF16, tag="bank")
             for t in range(PACK):
                 nc.tensor.transpose(xT_bank[:, t, :], x_sb[:, PACK * g + t, :], ident_bf16[:])
-            nc.scalar.copy(out=xT_sb[:, g], in_=xT_bank[:])
+            copy_out(g % 2 == 0, xT_sb[:, g], xT_bank[:])
 
         def multiply_x(g):
             w_sb = we_sb if g < E_PASSES else wf_sb
@@ -110,7 +111,7 @@ def tile_two_d_cxn_cmps_pb_kernel(tc, xe, xf, Ge2f, Gf2f, We2f, Wf2f, out):
                 nc.tensor.matmul(
                     h_bank[:, t, :], lhsT=xT_sb[:, g, t, :], rhs=w_sb[:], start=True, stop=True
                 )
-            copy_out(g % 2 == 1, h_grouped[:, g], h_bank[:].rearrange("p t d -> p d t"))
+            copy_out(g % 2 == 0, h_grouped[:, g], h_bank[:].rearrange("p t d -> p d t"))
 
         def quantise_h(c):
             cols = slice(c * STEP_WORDS, (c + 1) * STEP_WORDS)
@@ -135,24 +136,23 @@ def tile_two_d_cxn_cmps_pb_kernel(tc, xe, xf, Ge2f, Gf2f, We2f, Wf2f, out):
         grouped_of = {}
         quantised = {}
 
-        def sorted_passes(r):
-            return 6 if r < 2 else 8
-
-        def sort_words(r):
-            passes = sorted_passes(r)
-            tile = sorted_pool.tile([P, passes * WORDS_PASS], F32)
-            sorted_words[r] = tile
+        def sort_words(r, c):
+            first, end = SORTS[c]
+            tile = sorted_pool.tile([P, (end - first) * WORDS_PASS], F32)
+            for g in range(first, end):
+                sorted_words[(r, g)] = (tile, g - first)
             nc.vector.tensor_copy(
-                out=tile[:].rearrange("p (g u w) -> p g u w", g=passes, u=2),
-                in_=g_words[r][:, : passes * WORDS_PASS].rearrange(
-                    "p (g w u) -> p g u w", g=passes, u=2
+                out=tile[:].rearrange("p (g u w) -> p g u w", g=end - first, u=2),
+                in_=g_words[r][:, first * WORDS_PASS : end * WORDS_PASS].rearrange(
+                    "p (g w u) -> p g u w", g=end - first, u=2
                 ),
             )
 
         def words_of(r, g, u):
-            if g < sorted_passes(r):
-                first = (2 * g + u) * P
-                return sorted_words[r][:, first : first + P]
+            if (r, g) in sorted_words:
+                tile, place = sorted_words[(r, g)]
+                first = (2 * place + u) * P
+                return tile[:, first : first + P]
             return g_words[r][:, g * WORDS_PASS + u : (g + 1) * WORDS_PASS : 2]
 
         def transpose_step(s):
@@ -204,8 +204,8 @@ def tile_two_d_cxn_cmps_pb_kernel(tc, xe, xf, Ge2f, Gf2f, We2f, Wf2f, out):
 
         def advance(s):
             r, c = divmod(s + SORT_AHEAD, ROUND_STEPS)
-            if r < ROUNDS and c == 0:
-                sort_words(r)
+            if 1 <= r < ROUNDS and c in SORTS:
+                sort_words(r, c)
             if s >= 0:
                 transpose_step(s)
             if s >= 1:

@@ -51,7 +51,7 @@ def tile_two_d_cxn_cmps_pb_kernel(tc, xe, xf, Ge2f, Gf2f, We2f, Wf2f, out):
         sums = stack.enter_context(tc.psum_pool(name="sums", bufs=2))
         stack.enter_context(tc.manual_schedule())
 
-        x_sb = keep.tile([P, PASSES * PACK, D], BF16)
+        x_sb = keep.tile([P, PASSES * PACK, D], BF16, align_bytes=256)
         x_passes = x_sb[:].rearrange("p (g t) d -> p g t d", t=PACK)
         xe_passes = xe.rearrange("(g p t) d -> p g t d", p=P, t=PACK)
         xf_passes = xf.rearrange("(g p t) d -> p g t d", p=P, t=PACK)
@@ -73,7 +73,7 @@ def tile_two_d_cxn_cmps_pb_kernel(tc, xe, xf, Ge2f, Gf2f, We2f, Wf2f, out):
 
         def load_round(r):
             rows = slice(r * P, (r + 1) * P)
-            g_tile = g_pool.tile([P, N_E + N_F], BF16)
+            g_tile = g_pool.tile([P, N_E + N_F], BF16, align_bytes=256)
             nc.sync.dma_start(out=g_tile[:, :N_E], in_=Ge2f[rows, :])
             nc.sync.dma_start(out=g_tile[:, N_E:], in_=Gf2f[rows, :])
             return g_tile[:].bitcast(F32)
@@ -134,6 +134,7 @@ def tile_two_d_cxn_cmps_pb_kernel(tc, xe, xf, Ge2f, Gf2f, We2f, Wf2f, out):
             unit_of[s] = (len(units) - 1, s - units[-1][0])
         sorted_words = {}
         grouped_of = {}
+        unstored = []
         quantised = {}
 
         def sort_words(r, c):
@@ -200,7 +201,11 @@ def tile_two_d_cxn_cmps_pb_kernel(tc, xe, xf, Ge2f, Gf2f, We2f, Wf2f, out):
                 )
             z = z_pool.tile([P, D], F32)
             copy_out(r % 2 == 0, z[:], acc[:])
-            nc.sync.dma_start(out=out[r * P : (r + 1) * P, :], in_=z[:])
+            unstored.append((r, z))
+            if len(g_words) == ROUNDS:
+                for q, z_of_q in unstored:
+                    nc.sync.dma_start(out=out[q * P : (q + 1) * P, :], in_=z_of_q[:])
+                unstored.clear()
 
         def advance(s):
             r, c = divmod(s + SORT_AHEAD, ROUND_STEPS)

@@ -31,7 +31,7 @@ X_AHEAD = 2
 G_START = 7
 SORT_AHEAD = 5
 SORTS = {1: (2, E_PASSES), 3: (E_PASSES, PASSES)}
-MX_LAG = 8
+MX_LAG = 6
 G_BUFS = 12
 WORK_BANKS = 6
 
@@ -171,7 +171,7 @@ def tile_two_d_cxn_cmps_pb_kernel(tc, xe, xf, Ge2f, Gf2f, We2f, Wf2f, out):
             cols = slice(place * STEP_COLS, (place + 1) * STEP_COLS)
             dst = grouped_of[j][:, cols].bitcast(F32)
             dst = dst.rearrange("p (i r u) -> p i r u", i=STEP_PASSES, u=2)
-            nc.scalar.copy(out=dst, in_=bank[:].rearrange("p i u r -> p i r u"))
+            copy_out(s != STEPS - ROUND_STEPS + 1, dst, bank[:].rearrange("p i u r -> p i r u"))
 
         def quantise_unit(j):
             words = units[j][1] * STEP_WORDS
@@ -209,7 +209,7 @@ def tile_two_d_cxn_cmps_pb_kernel(tc, xe, xf, Ge2f, Gf2f, We2f, Wf2f, out):
 
         def advance(s):
             r, c = divmod(s + SORT_AHEAD, ROUND_STEPS)
-            if 1 <= r < ROUNDS and c in SORTS:
+            if 1 <= r < ROUNDS and c in SORTS and not (r == ROUNDS - 1 and c == 3):
                 sort_words(r, c)
             if s >= 0:
                 transpose_step(s)

@@ -226,14 +226,17 @@ def tile_two_d_cxn_cmps_pb_kernel(tc, xe, xf, Ge2f, Gf2f, We2f, Wf2f, out):
 
         for g in range(X_AHEAD):
             transpose_x(g)
-        for g in range(PASSES):
-            if g + X_AHEAD < PASSES:
-                transpose_x(g + X_AHEAD)
-            multiply_x(g)
-            if g % STEP_PASSES == STEP_PASSES - 1 and g // STEP_PASSES >= 1:
+        for g in range(0, PASSES, STEP_PASSES):
+            for i in range(STEP_PASSES):
+                if g + i + X_AHEAD < PASSES:
+                    transpose_x(g + i + X_AHEAD)
+            for i in range(STEP_PASSES):
+                multiply_x(g + i)
+            if g >= STEP_PASSES:
                 quantise_h(g // STEP_PASSES - 1)
-            if g >= G_START - SORT_AHEAD:
-                advance(g - G_START)
+            for i in range(STEP_PASSES):
+                if g + i >= G_START - SORT_AHEAD:
+                    advance(g + i - G_START)
         quantise_h(PASSES // STEP_PASSES - 1)
         for s in range(PASSES - G_START, STEPS):
             advance(s)

from contextlib import ExitStack

import concourse.mybir as mybir
from concourse.masks import make_identity

BF16 = mybir.dt.bfloat16
F32 = mybir.dt.float32
U32 = mybir.dt.uint32
U8 = mybir.dt.uint8
FP8X4 = mybir.dt.float8_e4m3fn_x4

P = 128
PACK = 4
K_PASS = P * PACK
N_E, N_F, D = 3072, 2048, 128
E_PASSES = N_E // K_PASS
F_PASSES = N_F // K_PASS
PASSES = E_PASSES + F_PASSES
WORDS_PASS = K_PASS // 2
ROUNDS = N_F // P

STEP_PASSES = 2
ROUND_STEPS = PASSES // STEP_PASSES
STEPS = ROUNDS * ROUND_STEPS
STEP_COLS = STEP_PASSES * K_PASS
STEP_WORDS = STEP_COLS // PACK
UNIT_STEPS = 2
ALONE_STEPS = 4

X_AHEAD = 2
G_START = 7
SORT_AHEAD = 5
SORTS = {1: (2, E_PASSES), 3: (E_PASSES, PASSES)}
MX_LAG = 6
G_BUFS = 12
WORK_BANKS = 6

FLOPS = 2 * N_F * (N_E + N_F) * D + 2 * (N_E + N_F) * D * D


def tile_two_d_cxn_cmps_pb_kernel(tc, xe, xf, Ge2f, Gf2f, We2f, Wf2f, out):
    nc = tc.nc
    with ExitStack() as stack:
        keep = stack.enter_context(tc.tile_pool(name="keep", bufs=1))
        g_pool = stack.enter_context(tc.tile_pool(name="g", bufs=G_BUFS))
        sorted_pool = stack.enter_context(tc.tile_pool(name="sorted", bufs=4))
        grouped_pool = stack.enter_context(tc.tile_pool(name="grouped", bufs=4))
        quantised_pool = stack.enter_context(tc.tile_pool(name="quantised", bufs=10))
        z_pool = stack.enter_context(tc.tile_pool(name="z", bufs=ROUNDS))
        work = stack.enter_context(tc.psum_pool(name="work", bufs=WORK_BANKS))
        sums = stack.enter_context(tc.psum_pool(name="sums", bufs=2))
        stack.enter_context(tc.manual_schedule())

        x_sb = keep.tile([P, PASSES * PACK, D], BF16, align_bytes=256)
        x_passes = x_sb[:].rearrange("p (g t) d -> p g t d", t=PACK)
        xe_passes = xe.rearrange("(g p t) d -> p g t d", p=P, t=PACK)
        xf_passes = xf.rearrange("(g p t) d -> p g t d", p=P, t=PACK)

        def load_x(g, passes):
            src, first = (xe_passes, g) if g < E_PASSES else (xf_passes, g - E_PASSES)
            nc.sync.dma_start(
                out=x_passes[:, g : g + passes], in_=src[:, first : first + passes]
            )

        load_x(0, 1)
        we_sb = keep.tile([P, D], BF16)
        nc.sync.dma_start(out=we_sb[:], in_=We2f)
        wf_sb = keep.tile([P, D], BF16)
        nc.sync.dma_start(out=wf_sb[:], in_=Wf2f)
        load_x(1, 1)
        for g in range(2, PASSES, 2):
            load_x(g, 2)

        def load_round(r):
            rows = slice(r * P, (r + 1) * P)
            g_tile = g_pool.tile([P, N_E + N_F], BF16, align_bytes=256)
            nc.sync.dma_start(out=g_tile[:, :N_E], in_=Ge2f[rows, :])
            nc.sync.dma_start(out=g_tile[:, N_E:], in_=Gf2f[rows, :])
            return g_tile[:].bitcast(F32)

        g_words = {}
        for r in range(G_BUFS):
            g_words[r] = load_round(r)

        ident_bf16 = keep.tile([P, P], BF16)
        make_identity(nc, ident_bf16[:])
        ident_f32 = keep.tile([P, P], F32)
        make_identity(nc, ident_f32[:])

        xT_sb = keep.tile([P, PASSES, PACK, P], BF16)
        h_grouped = keep.tile([P, PASSES, D, PACK], BF16, align_bytes=64)
        h_codes = keep.tile([P, PASSES * D], U32, align_bytes=64)
        h_scales = keep.tile([P, PASSES * D], U8, align_bytes=64)

        def copy_out(on_scalar, dst, src):
            if on_scalar:
                nc.scalar.copy(out=dst, in_=src)
            else:
                nc.vector.tensor_copy(out=dst, in_=src)

        def transpose_x(g):
            xT_bank = work.tile([P, PACK, P], BF16, tag="bank")
            for t in range(PACK):
                nc.tensor.transpose(xT_bank[:, t, :], x_sb[:, PACK * g + t, :], ident_bf16[:])
            copy_out(g % 2 == 0, xT_sb[:, g], xT_bank[:])

        def multiply_x(g):
            w_sb = we_sb if g < E_PASSES else wf_sb
            h_bank = work.tile([P, PACK, D], F32, tag="bank")
            for t in range(PACK):
                nc.tensor.matmul(
                    h_bank[:, t, :], lhsT=xT_sb[:, g, t, :], rhs=w_sb[:], start=True, stop=True
                )
            copy_out(g % 2 == 0, h_grouped[:, g], h_bank[:].rearrange("p t d -> p d t"))

        def quantise_h(c):
            cols = slice(c * STEP_WORDS, (c + 1) * STEP_WORDS)
            nc.vector.quantize_mx(
                out=h_codes[:, cols].bitcast(FP8X4),
                scales=h_scales[:, cols],
                in_=h_grouped[:, c * STEP_PASSES : (c + 1) * STEP_PASSES].rearrange(
                    "p g d t -> p (g d t)"
                ),
            )

        units = []
        unit_of = {}
        for s in range(STEPS):
            first, steps = units[-1] if units else (0, UNIT_STEPS)
            if not units or steps == UNIT_STEPS or s >= STEPS - ALONE_STEPS:
                units.append((s, 1))
            else:
                units[-1] = (first, steps + 1)
            unit_of[s] = (len(units) - 1, s - units[-1][0])
        sorted_words = {}
        grouped_of = {}
        unstored = []
        quantised = {}

        def sort_words(r, c):
            first, end = SORTS[c]
            tile = sorted_pool.tile([P, (end - first) * WORDS_PASS], F32)
            for g in range(first, end):
                sorted_words[(r, g)] = (tile, g - first)
            nc.vector.tensor_copy(
                out=tile[:].rearrange("p (g u w) -> p g u w", g=end - first, u=2),
                in_=g_words[r][:, first * WORDS_PASS : end * WORDS_PASS].rearrange(
                    "p (g w u) -> p g u w", g=end - first, u=2
                ),
            )

        def words_of(r, g, u):
            if (r, g) in sorted_words:
                tile, place = sorted_words[(r, g)]
                first = (2 * place + u) * P
                return tile[:, first : first + P]
            return g_words[r][:, g * WORDS_PASS + u : (g + 1) * WORDS_PASS : 2]

        def transpose_step(s):
            r, c = divmod(s, ROUND_STEPS)
            bank = work.tile([P, STEP_PASSES, 2, P], F32, tag="bank")
            for i in range(STEP_PASSES):
                for u in range(2):
                    nc.tensor.transpose(
                        bank[:, i, u, :], words_of(r, c * STEP_PASSES + i, u), ident_f32[:]
                    )
            j, place = unit_of[s]
            if place == 0:
                grouped = grouped_pool.tile([P, units[j][1] * STEP_COLS], BF16, align_bytes=64)
                grouped_of[j] = grouped
            cols = slice(place * STEP_COLS, (place + 1) * STEP_COLS)
            dst = grouped_of[j][:, cols].bitcast(F32)
            dst = dst.rearrange("p (i r u) -> p i r u", i=STEP_PASSES, u=2)
            copy_out(s != STEPS - ROUND_STEPS + 1, dst, bank[:].rearrange("p i u r -> p i r u"))

        def quantise_unit(j):
            words = units[j][1] * STEP_WORDS
            codes = quantised_pool.tile([P, words], U32, align_bytes=64)
            scales = quantised_pool.tile([P, words], U8, align_bytes=64)
            quantised[j] = (codes, scales)
            nc.vector.quantize_mx(
                out=codes[:].bitcast(FP8X4), scales=scales[:], in_=grouped_of[j][:]
            )

        def multiply_round(r):
            acc = sums.tile([P, D], F32)
            for g in range(PASSES):
                c, i = divmod(g, STEP_PASSES)
                j, place = unit_of[r * ROUND_STEPS + c]
                codes, scales = quantised[j]
                first = (place * STEP_PASSES + i) * P
                h_cols = slice(g * D, (g + 1) * D)
                nc.tensor.matmul_mx(
                    out=acc[:],
                    lhsT=codes[:, first : first + P].bitcast(FP8X4),
                    lhsT_scale=scales[:, first : first + P],
                    rhs=h_codes[:, h_cols].bitcast(FP8X4),
                    rhs_scale=h_scales[:, h_cols],
                    start=(g == 0),
                    stop=(g == PASSES - 1),
                )
            z = z_pool.tile([P, D], F32)
            copy_out(r % 2 == 0, z[:], acc[:])
            unstored.append((r, z))
            if len(g_words) == ROUNDS:
                for q, z_of_q in unstored:
                    nc.sync.dma_start(out=out[q * P : (q + 1) * P, :], in_=z_of_q[:])
                unstored.clear()

        def advance(s):
            r, c = divmod(s + SORT_AHEAD, ROUND_STEPS)
            if 1 <= r < ROUNDS and c in SORTS and not (r == ROUNDS - 1 and c == 3):
                sort_words(r, c)
            if s >= 0:
                transpose_step(s)
            if s >= 1:
                j, place = unit_of[s - 1]
                if place == units[j][1] - 1:
                    quantise_unit(j)
            r, c = divmod(s - MX_LAG, ROUND_STEPS)
            if r >= 0 and c == ROUND_STEPS - 1:
                multiply_round(r)
            r, c = divmod(s, ROUND_STEPS)
            if r >= 0 and c == ROUND_STEPS - 1 and r + G_BUFS < ROUNDS:
                g_words[r + G_BUFS] = load_round(r + G_BUFS)

        for g in range(X_AHEAD):
            transpose_x(g)
        for g in range(0, PASSES, STEP_PASSES):
            for i in range(STEP_PASSES):
                if g + i + X_AHEAD < PASSES:
                    transpose_x(g + i + X_AHEAD)
            for i in range(STEP_PASSES):
                multiply_x(g + i)
            if g >= STEP_PASSES:
                quantise_h(g // STEP_PASSES - 1)
            for i in range(STEP_PASSES):
                if g + i >= G_START - SORT_AHEAD:
                    advance(g + i - G_START)
        quantise_h(PASSES // STEP_PASSES - 1)
        for s in range(PASSES - G_START, STEPS):
            advance(s)
        quantise_unit(len(units) - 1)
        for r in range((STEPS - MX_LAG) // ROUND_STEPS, ROUNDS):
            multiply_round(r)
